import numpy as np
import ml_dtypes

BF16 = ml_dtypes.bfloat16


def bf(x):
    return np.asarray(x, np.float32).astype(BF16)


def f32(x):
    return np.asarray(x, np.float32)


def f64(x):
    return np.asarray(x).astype(np.float64)


def striped(idx):
    return np.tile(idx.reshape(-1, 16).T, (8, 1))


C, S, N, K, A, P, L, R = 1024, 512, 256, 2, 4, 256, 128, 3

QKV_SCALE = np.array([[0.05], [0.05], [1.0]])


def setup_inputs():
    return {
        "xq": f32(np.random.standard_normal((C, N))),
        "xk": f32(np.random.standard_normal((C, N))),
        "xv": f32(np.random.standard_normal((C, N))),
        "w_qkv": f32(QKV_SCALE * np.random.standard_normal((R, N))),
        "b_qkv": f32(QKV_SCALE * np.random.standard_normal((R, N))),
        "w_up": f32(np.random.standard_normal((A, N))),
        "b_up": f32(0.3 * np.random.standard_normal((1, N))),
        "base": f32(np.random.standard_normal((C, S))),
        "offs": striped(np.random.permutation(S)[:N]),
    }


def reference(xq, xk, xv, w_qkv, b_qkv, w_up, b_up, base, offs):
    idx = offs[:16].T.reshape(-1)
    w, b = f64(w_qkv), f64(b_qkv)
    q = f64(xq).reshape(A, P, N).max(axis=0) * w[0] + b[0]
    k = f64(xk).reshape(A, P, N).max(axis=0) * w[1] + b[1]
    v = f64(xv).reshape(A, P, N).max(axis=0) * w[2] + b[2]
    o = np.zeros((P, N))
    for t in range(K):
        sl = slice(t * L, (t + 1) * L)
        sc = q[:, sl].T @ k[:, sl]
        e = np.exp(sc - sc.max(axis=1, keepdims=True))
        att = e / e.sum(axis=1, keepdims=True)
        o[:, sl] = v[:, sl] @ att.T
    up = (o[None, :, :] * f64(w_up)[:, None, :]).reshape(C, N) + f64(b_up)
    out = f64(base).copy()
    out[:, idx] = up
    return out

@@ -1,0 +1,156 @@
+import concourse.mybir as mybir
+from concourse.masks import make_identity
+
+F32 = mybir.dt.float32
+BF16 = mybir.dt.bfloat16
+U16 = mybir.dt.uint16
+ALU = mybir.AluOpType
+ACT = mybir.ActivationFunctionType
+AXIS = mybir.AxisListType
+
+PARTS = 128
+A = 4
+H = 2
+N = 256
+T = 2
+L = 128
+S = 512
+
+FLOPS = 2 * (2 * T * L * L * PARTS * H)
+
+
+def load_maps(nc, pool, x, label):
+    maps = []
+    for a in range(A):
+        rows = x[a * H * PARTS : (a + 1) * H * PARTS, :]
+        one = pool.tile([PARTS, H, N], F32, name=f"{label}{a}")
+        nc.sync.dma_start(one[:], rows.rearrange("(p h) n -> p h n", h=H))
+        maps.append(one)
+    return maps
+
+
+def max_over_positions(nc, pool, maps, label):
+    pooled = pool.tile([PARTS, H, N], F32, name=label)
+    nc.vector.tensor_max(pooled[:], maps[0][:], maps[1][:])
+    for one in maps[2:]:
+        nc.vector.tensor_max(pooled[:], pooled[:], one[:])
+    return pooled
+
+
+def gain_bias_rounded(nc, pool, pooled, spread, label):
+    gain = spread[:, 0:N].unsqueeze(1).to_broadcast([PARTS, H, N])
+    bias = spread[:, N : 2 * N].unsqueeze(1).to_broadcast([PARTS, H, N])
+    scaled = pool.tile([PARTS, H, N], F32, name=f"{label}_scaled")
+    nc.vector.tensor_tensor(scaled[:], pooled[:], gain, ALU.mult)
+    rounded = pool.tile([PARTS, H, N], BF16, name=label)
+    nc.vector.tensor_tensor(rounded[:], scaled[:], bias, ALU.add)
+    return rounded
+
+
+def tile_clusterlocalatt_kernel(tc, xq, xk, xv, w_qkv, b_qkv, w_up, b_up, base, offs, out):
+    nc = tc.nc
+    with (
+        tc.tile_pool(name="held", bufs=1) as held,
+        tc.tile_pool(name="ring", bufs=2) as ring,
+        tc.psum_pool(name="psum", bufs=1) as psum,
+    ):
+        offsets = held.tile([PARTS, N // 16], U16, name="offsets")
+        nc.sync.dma_start(offsets[:], offs)
+
+        params = held.tile([1, 6 * N], F32, name="params")
+        nc.scalar.dma_start(params[:, 0 : 3 * N], w_qkv.rearrange("(o r) n -> o (r n)", o=1))
+        nc.scalar.dma_start(params[:, 3 * N : 6 * N], b_qkv.rearrange("(o r) n -> o (r n)", o=1))
+
+        ones = held.tile([1, PARTS], F32, name="ones")
+        nc.vector.memset(ones[:], 1.0)
+        ident_f32 = held.tile([PARTS, PARTS], F32, name="ident_f32")
+        make_identity(nc, ident_f32[:])
+        ident_bf16 = held.tile([PARTS, PARTS], BF16, name="ident_bf16")
+        make_identity(nc, ident_bf16[:])
+
+        warm = held.tile([PARTS, 1], F32, name="warm")
+        nc.vector.memset(warm[:], 0.0)
+        nc.scalar.activation(warm[:], warm[:], ACT.Exp)
+
+        maps_q = load_maps(nc, held, xq, "xq")
+        maps_k = load_maps(nc, held, xk, "xk")
+        maps_v = load_maps(nc, held, xv, "xv")
+        w_up_all = held.tile([PARTS, A * N], F32, name="w_up_all")
+        nc.sync.dma_start(w_up_all[:], w_up.rearrange("a n -> (a n)").partition_broadcast(PARTS))
+        b_up_all = held.tile([PARTS, N], F32, name="b_up_all")
+        nc.sync.dma_start(b_up_all[:], b_up.rearrange("o n -> (o n)").partition_broadcast(PARTS))
+        base_blocks = base.rearrange("(a p h) s -> a h p s", a=A, h=H)
+        out_blocks = out.rearrange("(a p h) s -> a h p s", a=A, h=H)
+        windows = {}
+        for h in range(H):
+            for a in range(A):
+                windows[a, h] = held.tile([PARTS, S], F32, name=f"window{a}{h}")
+                nc.sync.dma_start(windows[a, h][:], base_blocks[a, h])
+
+        spread = {}
+        for r, label in enumerate(("q", "k")):
+            spread[label] = psum.tile([PARTS, 2 * N], F32, name=f"spread_{label}")
+            nc.tensor.matmul(spread[label][:, 0:N], ones[:], params[:, r * N : (r + 1) * N], start=True, stop=True)
+            nc.tensor.matmul(
+                spread[label][:, N : 2 * N], ones[:], params[:, (3 + r) * N : (4 + r) * N], start=True, stop=True
+            )
+        v_cols_psum = psum.tile([PARTS, 2 * T], F32, name="v_cols_psum")
+        for t in range(T):
+            gain_row = params[:, 2 * N + t * L : 2 * N + (t + 1) * L]
+            bias_row = params[:, 5 * N + t * L : 5 * N + (t + 1) * L]
+            nc.tensor.matmul(v_cols_psum[:, t : t + 1], gain_row, ones[:, 0:1], start=True, stop=True)
+            nc.tensor.matmul(v_cols_psum[:, T + t : T + t + 1], bias_row, ones[:, 0:1], start=True, stop=True)
+        v_cols = held.tile([PARTS, 2 * T], F32, name="v_cols")
+        nc.vector.tensor_copy(v_cols[:], v_cols_psum[:])
+
+        q = gain_bias_rounded(nc, held, max_over_positions(nc, held, maps_q, "pooled_q"), spread["q"], "q")
+        k = gain_bias_rounded(nc, held, max_over_positions(nc, held, maps_k, "pooled_k"), spread["k"], "k")
+
+        score = psum.tile([PARTS, T, L], F32, name="score")
+        for t in range(T):
+            cluster = slice(t * L, (t + 1) * L)
+            for h in range(H):
+                nc.tensor.matmul(
+                    score[:, t, :], q[:, h, cluster], k[:, h, cluster], start=(h == 0), stop=(h == H - 1)
+                )
+
+        negmax = held.tile([PARTS, T], F32, name="negmax")
+        nc.vector.tensor_reduce(negmax[:], score[:], AXIS.X, ALU.max, negate=True)
+        e = held.tile([PARTS, T, L], F32, name="e")
+        esum = held.tile([PARTS, T], F32, name="esum")
+        for t in range(T):
+            nc.scalar.activation(
+                e[:, t, :], score[:, t, :], ACT.Exp, bias=negmax[:, t : t + 1], scale=1.0, accum_out=esum[:, t : t + 1]
+            )
+        rsum = held.tile([PARTS, T], F32, name="rsum")
+        nc.vector.reciprocal(rsum[:], esum[:])
+        att = held.tile([PARTS, T, L], BF16, name="att")
+        for t in range(T):
+            nc.scalar.mul(att[:, t, :], e[:, t, :], rsum[:, t : t + 1])
+
+        attT_psum = psum.tile([PARTS, T, L], BF16, name="attT_psum")
+        for t in range(T):
+            nc.tensor.transpose(attT_psum[:, t, :], att[:, t, :], ident_bf16[:])
+        attT = held.tile([PARTS, T, L], BF16, name="attT")
+        nc.scalar.copy(attT[:], attT_psum[:])
+
+        pooled_v = max_over_positions(nc, held, maps_v, "pooled_v")
+        vT_psum = psum.tile([PARTS, T, H, PARTS], F32, name="vT_psum")
+        for t in range(T):
+            for h in range(H):
+                nc.tensor.transpose(vT_psum[:, t, h, :], pooled_v[:, h, t * L : (t + 1) * L], ident_f32[:])
+        vT = held.tile([PARTS, T, H, PARTS], BF16, name="vT")
+        for t in range(T):
+            nc.scalar.activation(
+                vT[:, t], vT_psum[:, t], ACT.Identity, bias=v_cols[:, T + t : T + t + 1], scale=v_cols[:, t : t + 1]
+            )
+
+        for h in range(H):
+            o = psum.tile([PARTS, N], F32, name=f"o{h}")
+            for t in range(T):
+                nc.tensor.matmul(o[:, t * L : (t + 1) * L], vT[:, t, h, :], attT[:, t, :], start=True, stop=True)
+            for a in range(A):
+                product = ring.tile([PARTS, N], F32, name="product")
+                nc.vector.tensor_tensor(product[:], o[:], w_up_all[:, a * N : (a + 1) * N], ALU.mult)
+                nc.vector.tensor_tensor(windows[a, h][:].indirect(offsets[:]), product[:], b_up_all[:], ALU.add)
+                nc.sync.dma_start(out_blocks[a, h], windows[a, h][:])

@@ -20,28 +20,29 @@ FLOPS = 2 * (2 * T * L * L * PARTS * H)
 
 
 def load_maps(nc, pool, x, label):
-    maps = []
-    for a in range(A):
-        rows = x[a * H * PARTS : (a + 1) * H * PARTS, :]
-        one = pool.tile([PARTS, H, N], F32, name=f"{label}{a}")
-        nc.sync.dma_start(one[:], rows.rearrange("(p h) n -> p h n", h=H))
-        maps.append(one)
-    return maps
+    by_position = x.rearrange("(a p h) n -> p a (h n)", a=A, h=H)
+    halves = []
+    for half, queue in enumerate((nc.sync, nc.scalar)):
+        two = pool.tile([PARTS, A // 2, H * N], F32, name=f"{label}{half}")
+        queue.dma_start(two[:], by_position[:, half * (A // 2) : (half + 1) * (A // 2), :])
+        halves.append(two)
+    return halves
 
 
-def max_over_positions(nc, pool, maps, label):
-    pooled = pool.tile([PARTS, H, N], F32, name=label)
-    nc.vector.tensor_max(pooled[:], maps[0][:], maps[1][:])
-    for one in maps[2:]:
-        nc.vector.tensor_max(pooled[:], pooled[:], one[:])
-    return pooled
+def max_over_positions(nc, pool, halves, label):
+    pooled = pool.tile([PARTS, H * N], F32, name=label)
+    other = pool.tile([PARTS, H * N], F32, name=f"{label}_other")
+    nc.vector.tensor_max(pooled[:], halves[0][:, 0, :], halves[0][:, 1, :])
+    nc.vector.tensor_max(other[:], halves[1][:, 0, :], halves[1][:, 1, :])
+    nc.vector.tensor_max(pooled[:], pooled[:], other[:])
+    return pooled.rearrange("p (h n) -> p h n", h=H)
 
 
 def gain_bias_rounded(nc, pool, pooled, spread, label):
     gain = spread[:, 0:N].unsqueeze(1).to_broadcast([PARTS, H, N])
     bias = spread[:, N : 2 * N].unsqueeze(1).to_broadcast([PARTS, H, N])
     scaled = pool.tile([PARTS, H, N], F32, name=f"{label}_scaled")
-    nc.vector.tensor_tensor(scaled[:], pooled[:], gain, ALU.mult)
+    nc.vector.tensor_tensor(scaled[:], pooled, gain, ALU.mult)
     rounded = pool.tile([PARTS, H, N], BF16, name=label)
     nc.vector.tensor_tensor(rounded[:], scaled[:], bias, ALU.add)
     return rounded
@@ -62,14 +63,14 @@ def tile_clusterlocalatt_kernel(tc, xq, xk, xv, w_qkv, b_qkv, w_up, b_up, base, 
         nc.scalar.dma_start(params[:, 3 * N : 6 * N], b_qkv.rearrange("(o r) n -> o (r n)", o=1))
 
         ones = held.tile([1, PARTS], F32, name="ones")
-        nc.vector.memset(ones[:], 1.0)
+        nc.gpsimd.memset(ones[:], 1.0)
         ident_f32 = held.tile([PARTS, PARTS], F32, name="ident_f32")
         make_identity(nc, ident_f32[:])
         ident_bf16 = held.tile([PARTS, PARTS], BF16, name="ident_bf16")
         make_identity(nc, ident_bf16[:])
 
         warm = held.tile([PARTS, 1], F32, name="warm")
-        nc.vector.memset(warm[:], 0.0)
+        nc.gpsimd.memset(warm[:], 0.0)
         nc.scalar.activation(warm[:], warm[:], ACT.Exp)
 
         maps_q = load_maps(nc, held, xq, "xq")
@@ -78,14 +79,15 @@ def tile_clusterlocalatt_kernel(tc, xq, xk, xv, w_qkv, b_qkv, w_up, b_up, base, 
         w_up_all = held.tile([PARTS, A * N], F32, name="w_up_all")
         nc.sync.dma_start(w_up_all[:], w_up.rearrange("a n -> (a n)").partition_broadcast(PARTS))
         b_up_all = held.tile([PARTS, N], F32, name="b_up_all")
-        nc.sync.dma_start(b_up_all[:], b_up.rearrange("o n -> (o n)").partition_broadcast(PARTS))
+        nc.scalar.dma_start(b_up_all[:], b_up.rearrange("o n -> (o n)").partition_broadcast(PARTS))
         base_blocks = base.rearrange("(a p h) s -> a h p s", a=A, h=H)
         out_blocks = out.rearrange("(a p h) s -> a h p s", a=A, h=H)
+        queues = (nc.sync, nc.scalar)
         windows = {}
         for h in range(H):
             for a in range(A):
                 windows[a, h] = held.tile([PARTS, S], F32, name=f"window{a}{h}")
-                nc.sync.dma_start(windows[a, h][:], base_blocks[a, h])
+                queues[a % 2].dma_start(windows[a, h][:], base_blocks[a, h])
 
         spread = {}
         for r, label in enumerate(("q", "k")):
@@ -101,7 +103,7 @@ def tile_clusterlocalatt_kernel(tc, xq, xk, xv, w_qkv, b_qkv, w_up, b_up, base, 
             nc.tensor.matmul(v_cols_psum[:, t : t + 1], gain_row, ones[:, 0:1], start=True, stop=True)
             nc.tensor.matmul(v_cols_psum[:, T + t : T + t + 1], bias_row, ones[:, 0:1], start=True, stop=True)
         v_cols = held.tile([PARTS, 2 * T], F32, name="v_cols")
-        nc.vector.tensor_copy(v_cols[:], v_cols_psum[:])
+        nc.scalar.copy(v_cols[:], v_cols_psum[:])
 
         q = gain_bias_rounded(nc, held, max_over_positions(nc, held, maps_q, "pooled_q"), spread["q"], "q")
         k = gain_bias_rounded(nc, held, max_over_positions(nc, held, maps_k, "pooled_k"), spread["k"], "k")
@@ -153,4 +155,4 @@ def tile_clusterlocalatt_kernel(tc, xq, xk, xv, w_qkv, b_qkv, w_up, b_up, base, 
                 product = ring.tile([PARTS, N], F32, name="product")
                 nc.vector.tensor_tensor(product[:], o[:], w_up_all[:, a * N : (a + 1) * N], ALU.mult)
                 nc.vector.tensor_tensor(windows[a, h][:].indirect(offsets[:]), product[:], b_up_all[:], ALU.add)
-                nc.sync.dma_start(out_blocks[a, h], windows[a, h][:])
+                queues[a % 2].dma_start(out_blocks[a, h], windows[a, h][:])

@@ -15,6 +15,7 @@ N = 256
 T = 2
 L = 128
 S = 512
+BANK = 512
 
 FLOPS = 2 * (2 * T * L * L * PARTS * H)
 
@@ -54,13 +55,17 @@ def tile_clusterlocalatt_kernel(tc, xq, xk, xv, w_qkv, b_qkv, w_up, b_up, base, 
         tc.tile_pool(name="held", bufs=1) as held,
         tc.tile_pool(name="ring", bufs=2) as ring,
         tc.psum_pool(name="psum", bufs=1) as psum,
+        tc.psum_pool(name="banks", bufs=4) as banks,
     ):
         offsets = held.tile([PARTS, N // 16], U16, name="offsets")
         nc.sync.dma_start(offsets[:], offs)
 
-        params = held.tile([1, 6 * N], F32, name="params")
-        nc.scalar.dma_start(params[:, 0 : 3 * N], w_qkv.rearrange("(o r) n -> o (r n)", o=1))
-        nc.scalar.dma_start(params[:, 3 * N : 6 * N], b_qkv.rearrange("(o r) n -> o (r n)", o=1))
+        params = held.tile([1, 11 * N], F32, name="params")
+        gain_bias = params[:, 0 : 6 * N].rearrange("o (r g n) -> o r g n", g=2, n=N)
+        nc.scalar.dma_start(gain_bias[:, :, 0, :], w_qkv.rearrange("(o r) n -> o r n", o=1))
+        nc.scalar.dma_start(gain_bias[:, :, 1, :], b_qkv.rearrange("(o r) n -> o r n", o=1))
+        nc.scalar.dma_start(params[:, 6 * N : 10 * N], w_up.rearrange("(o a) n -> o (a n)", o=1))
+        nc.scalar.dma_start(params[:, 10 * N : 11 * N], b_up)
 
         ones = held.tile([1, PARTS], F32, name="ones")
         nc.gpsimd.memset(ones[:], 1.0)
@@ -76,37 +81,32 @@ def tile_clusterlocalatt_kernel(tc, xq, xk, xv, w_qkv, b_qkv, w_up, b_up, base, 
         maps_q = load_maps(nc, held, xq, "xq")
         maps_k = load_maps(nc, held, xk, "xk")
         maps_v = load_maps(nc, held, xv, "xv")
-        w_up_all = held.tile([PARTS, A * N], F32, name="w_up_all")
-        nc.sync.dma_start(w_up_all[:], w_up.rearrange("a n -> (a n)").partition_broadcast(PARTS))
-        b_up_all = held.tile([PARTS, N], F32, name="b_up_all")
-        nc.scalar.dma_start(b_up_all[:], b_up.rearrange("o n -> (o n)").partition_broadcast(PARTS))
         base_blocks = base.rearrange("(a p h) s -> a h p s", a=A, h=H)
         out_blocks = out.rearrange("(a p h) s -> a h p s", a=A, h=H)
-        queues = (nc.sync, nc.scalar)
         windows = {}
-        for h in range(H):
-            for a in range(A):
+        for a in range(A):
+            for h in range(H):
                 windows[a, h] = held.tile([PARTS, S], F32, name=f"window{a}{h}")
-                queues[a % 2].dma_start(windows[a, h][:], base_blocks[a, h])
+                nc.sync.dma_start(windows[a, h][:], base_blocks[a, h])
 
-        spread = {}
-        for r, label in enumerate(("q", "k")):
-            spread[label] = psum.tile([PARTS, 2 * N], F32, name=f"spread_{label}")
-            nc.tensor.matmul(spread[label][:, 0:N], ones[:], params[:, r * N : (r + 1) * N], start=True, stop=True)
-            nc.tensor.matmul(
-                spread[label][:, N : 2 * N], ones[:], params[:, (3 + r) * N : (4 + r) * N], start=True, stop=True
-            )
-        v_cols_psum = psum.tile([PARTS, 2 * T], F32, name="v_cols_psum")
-        for t in range(T):
-            gain_row = params[:, 2 * N + t * L : 2 * N + (t + 1) * L]
-            bias_row = params[:, 5 * N + t * L : 5 * N + (t + 1) * L]
-            nc.tensor.matmul(v_cols_psum[:, t : t + 1], gain_row, ones[:, 0:1], start=True, stop=True)
-            nc.tensor.matmul(v_cols_psum[:, T + t : T + t + 1], bias_row, ones[:, 0:1], start=True, stop=True)
-        v_cols = held.tile([PARTS, 2 * T], F32, name="v_cols")
-        nc.scalar.copy(v_cols[:], v_cols_psum[:])
+        spread_q = banks.tile([PARTS, BANK], F32, name="spread_q", tag="bank")
+        nc.tensor.matmul(spread_q[:], ones[:], params[:, 0 : 2 * N], start=True, stop=True)
+        spread_k = banks.tile([PARTS, BANK], F32, name="spread_k", tag="bank")
+        nc.tensor.matmul(spread_k[:], ones[:], params[:, 2 * N : 4 * N], start=True, stop=True)
+        n_cols = (2 + A) * T
+        cols_psum = banks.tile([PARTS, BANK], F32, name="cols_psum", tag="bank")
+        for c in range(n_cols):
+            piece = params[:, 4 * N + c * L : 4 * N + (c + 1) * L]
+            nc.tensor.matmul(cols_psum[:, c : c + 1], piece, ones[:, 0:1], start=True, stop=True)
+        cols = held.tile([PARTS, n_cols], F32, name="cols")
+        nc.scalar.copy(cols[:], cols_psum[:, 0:n_cols])
+        b_up_psum = banks.tile([PARTS, BANK], F32, name="b_up_psum", tag="bank")
+        nc.tensor.matmul(b_up_psum[:, 0:N], ones[:], params[:, 10 * N : 11 * N], start=True, stop=True)
+        b_up_all = held.tile([PARTS, N], F32, name="b_up_all")
+        nc.scalar.copy(b_up_all[:], b_up_psum[:, 0:N])
 
-        q = gain_bias_rounded(nc, held, max_over_positions(nc, held, maps_q, "pooled_q"), spread["q"], "q")
-        k = gain_bias_rounded(nc, held, max_over_positions(nc, held, maps_k, "pooled_k"), spread["k"], "k")
+        q = gain_bias_rounded(nc, held, max_over_positions(nc, held, maps_q, "pooled_q"), spread_q, "q")
+        k = gain_bias_rounded(nc, held, max_over_positions(nc, held, maps_k, "pooled_k"), spread_k, "k")
 
         score = psum.tile([PARTS, T, L], F32, name="score")
         for t in range(T):
@@ -137,22 +137,34 @@ def tile_clusterlocalatt_kernel(tc, xq, xk, xv, w_qkv, b_qkv, w_up, b_up, base, 
         nc.scalar.copy(attT[:], attT_psum[:])
 
         pooled_v = max_over_positions(nc, held, maps_v, "pooled_v")
-        vT_psum = psum.tile([PARTS, T, H, PARTS], F32, name="vT_psum")
+        vT_psum = psum.tile([PARTS, T, H * PARTS], F32, name="vT_psum")
         for t in range(T):
             for h in range(H):
-                nc.tensor.transpose(vT_psum[:, t, h, :], pooled_v[:, h, t * L : (t + 1) * L], ident_f32[:])
-        vT = held.tile([PARTS, T, H, PARTS], BF16, name="vT")
+                nc.tensor.transpose(
+                    vT_psum[:, t, h * PARTS : (h + 1) * PARTS], pooled_v[:, h, t * L : (t + 1) * L], ident_f32[:]
+                )
+        vT = held.tile([PARTS, T, H * PARTS], BF16, name="vT")
         for t in range(T):
             nc.scalar.activation(
-                vT[:, t], vT_psum[:, t], ACT.Identity, bias=v_cols[:, T + t : T + t + 1], scale=v_cols[:, t : t + 1]
+                vT[:, t, :], vT_psum[:, t, :], ACT.Identity, bias=cols[:, T + t : T + t + 1], scale=cols[:, t : t + 1]
             )
 
-        for h in range(H):
-            o = psum.tile([PARTS, N], F32, name=f"o{h}")
+        oT = psum.tile([PARTS, T, H * PARTS], F32, name="oT")
+        for t in range(T):
+            nc.tensor.matmul(oT[:, t, :], attT[:, t, :], vT[:, t, :], start=True, stop=True)
+
+        for a in range(A):
+            scaledT = ring.tile([PARTS, T, H * PARTS], F32, name="scaledT")
             for t in range(T):
-                nc.tensor.matmul(o[:, t * L : (t + 1) * L], vT[:, t, h, :], attT[:, t, :], start=True, stop=True)
-            for a in range(A):
+                w_up_col = cols[:, 2 * T + a * T + t : 2 * T + a * T + t + 1]
+                nc.scalar.mul(scaledT[:, t, :], oT[:, t, :], w_up_col)
+            for h in range(H):
+                flipped = banks.tile([PARTS, BANK], F32, name="flipped", tag="bank")
+                for t in range(T):
+                    nc.tensor.transpose(
+                        flipped[:, t * L : (t + 1) * L], scaledT[:, t, h * PARTS : (h + 1) * PARTS], ident_f32[:]
+                    )
                 product = ring.tile([PARTS, N], F32, name="product")
-                nc.vector.tensor_tensor(product[:], o[:], w_up_all[:, a * N : (a + 1) * N], ALU.mult)
+                nc.scalar.copy(product[:], flipped[:, 0:N])
                 nc.vector.tensor_tensor(windows[a, h][:].indirect(offsets[:]), product[:], b_up_all[:], ALU.add)
-                queues[a % 2].dma_start(out_blocks[a, h], windows[a, h][:])
+                nc.sync.dma_start(out_blocks[a, h], windows[a, h][:])

@@ -15,7 +15,6 @@ N = 256
 T = 2
 L = 128
 S = 512
-BANK = 512
 
 FLOPS = 2 * (2 * T * L * L * PARTS * H)
 
@@ -55,17 +54,16 @@ def tile_clusterlocalatt_kernel(tc, xq, xk, xv, w_qkv, b_qkv, w_up, b_up, base, 
         tc.tile_pool(name="held", bufs=1) as held,
         tc.tile_pool(name="ring", bufs=2) as ring,
         tc.psum_pool(name="psum", bufs=1) as psum,
-        tc.psum_pool(name="banks", bufs=4) as banks,
+        tc.psum_pool(name="banks", bufs=2) as banks,
     ):
         offsets = held.tile([PARTS, N // 16], U16, name="offsets")
         nc.sync.dma_start(offsets[:], offs)
 
         params = held.tile([1, 11 * N], F32, name="params")
-        gain_bias = params[:, 0 : 6 * N].rearrange("o (r g n) -> o r g n", g=2, n=N)
-        nc.scalar.dma_start(gain_bias[:, :, 0, :], w_qkv.rearrange("(o r) n -> o r n", o=1))
-        nc.scalar.dma_start(gain_bias[:, :, 1, :], b_qkv.rearrange("(o r) n -> o r n", o=1))
-        nc.scalar.dma_start(params[:, 6 * N : 10 * N], w_up.rearrange("(o a) n -> o (a n)", o=1))
-        nc.scalar.dma_start(params[:, 10 * N : 11 * N], b_up)
+        nc.scalar.dma_start(params[:, 0 : 3 * N], w_qkv.rearrange("(o r) n -> o (r n)", o=1))
+        nc.scalar.dma_start(params[:, 3 * N : 6 * N], b_qkv.rearrange("(o r) n -> o (r n)", o=1))
+        nc.sync.dma_start(params[:, 6 * N : 10 * N], w_up.rearrange("(o a) n -> o (a n)", o=1))
+        nc.sync.dma_start(params[:, 10 * N : 11 * N], b_up)
 
         ones = held.tile([1, PARTS], F32, name="ones")
         nc.gpsimd.memset(ones[:], 1.0)
@@ -83,30 +81,35 @@ def tile_clusterlocalatt_kernel(tc, xq, xk, xv, w_qkv, b_qkv, w_up, b_up, base, 
         maps_v = load_maps(nc, held, xv, "xv")
         base_blocks = base.rearrange("(a p h) s -> a h p s", a=A, h=H)
         out_blocks = out.rearrange("(a p h) s -> a h p s", a=A, h=H)
+        queues = (nc.sync, nc.scalar)
         windows = {}
-        for a in range(A):
-            for h in range(H):
+        for h in range(H):
+            for a in range(A):
                 windows[a, h] = held.tile([PARTS, S], F32, name=f"window{a}{h}")
-                nc.sync.dma_start(windows[a, h][:], base_blocks[a, h])
+                queues[a % 2].dma_start(windows[a, h][:], base_blocks[a, h])
 
-        spread_q = banks.tile([PARTS, BANK], F32, name="spread_q", tag="bank")
-        nc.tensor.matmul(spread_q[:], ones[:], params[:, 0 : 2 * N], start=True, stop=True)
-        spread_k = banks.tile([PARTS, BANK], F32, name="spread_k", tag="bank")
-        nc.tensor.matmul(spread_k[:], ones[:], params[:, 2 * N : 4 * N], start=True, stop=True)
-        n_cols = (2 + A) * T
-        cols_psum = banks.tile([PARTS, BANK], F32, name="cols_psum", tag="bank")
-        for c in range(n_cols):
-            piece = params[:, 4 * N + c * L : 4 * N + (c + 1) * L]
-            nc.tensor.matmul(cols_psum[:, c : c + 1], piece, ones[:, 0:1], start=True, stop=True)
-        cols = held.tile([PARTS, n_cols], F32, name="cols")
-        nc.scalar.copy(cols[:], cols_psum[:, 0:n_cols])
-        b_up_psum = banks.tile([PARTS, BANK], F32, name="b_up_psum", tag="bank")
-        nc.tensor.matmul(b_up_psum[:, 0:N], ones[:], params[:, 10 * N : 11 * N], start=True, stop=True)
+        spread = {}
+        for r, label in enumerate(("q", "k")):
+            spread[label] = banks.tile([PARTS, 2 * N], F32, name=f"spread_{label}", tag="bank")
+            nc.tensor.matmul(spread[label][:, 0:N], ones[:], params[:, r * N : (r + 1) * N], start=True, stop=True)
+            nc.tensor.matmul(
+                spread[label][:, N : 2 * N], ones[:], params[:, (3 + r) * N : (4 + r) * N], start=True, stop=True
+            )
+        v_cols_psum = psum.tile([PARTS, 2 * T], F32, name="v_cols_psum")
+        for t in range(T):
+            gain_row = params[:, 2 * N + t * L : 2 * N + (t + 1) * L]
+            bias_row = params[:, 5 * N + t * L : 5 * N + (t + 1) * L]
+            nc.tensor.matmul(v_cols_psum[:, t : t + 1], gain_row, ones[:, 0:1], start=True, stop=True)
+            nc.tensor.matmul(v_cols_psum[:, T + t : T + t + 1], bias_row, ones[:, 0:1], start=True, stop=True)
+        v_cols = held.tile([PARTS, 2 * T], F32, name="v_cols")
+        nc.scalar.copy(v_cols[:], v_cols_psum[:])
+        b_up_psum = psum.tile([PARTS, N], F32, name="b_up_psum")
+        nc.tensor.matmul(b_up_psum[:], ones[:], params[:, 10 * N : 11 * N], start=True, stop=True)
         b_up_all = held.tile([PARTS, N], F32, name="b_up_all")
-        nc.scalar.copy(b_up_all[:], b_up_psum[:, 0:N])
+        nc.scalar.copy(b_up_all[:], b_up_psum[:])
 
-        q = gain_bias_rounded(nc, held, max_over_positions(nc, held, maps_q, "pooled_q"), spread_q, "q")
-        k = gain_bias_rounded(nc, held, max_over_positions(nc, held, maps_k, "pooled_k"), spread_k, "k")
+        q = gain_bias_rounded(nc, held, max_over_positions(nc, held, maps_q, "pooled_q"), spread["q"], "q")
+        k = gain_bias_rounded(nc, held, max_over_positions(nc, held, maps_k, "pooled_k"), spread["k"], "k")
 
         score = psum.tile([PARTS, T, L], F32, name="score")
         for t in range(T):
@@ -115,6 +118,17 @@ def tile_clusterlocalatt_kernel(tc, xq, xk, xv, w_qkv, b_qkv, w_up, b_up, base, 
                 nc.tensor.matmul(
                     score[:, t, :], q[:, h, cluster], k[:, h, cluster], start=(h == 0), stop=(h == H - 1)
                 )
+
+        w_up_all = held.tile([PARTS, A * N], F32, name="w_up_all")
+        for pair in range(A // 2):
+            w_up_psum = banks.tile([PARTS, 2 * N], F32, name="w_up_psum", tag="bank")
+            for half in range(2):
+                a = 2 * pair + half
+                nc.tensor.matmul(
+                    w_up_psum[:, half * N : (half + 1) * N], ones[:], params[:, (6 + a) * N : (7 + a) * N],
+                    start=True, stop=True,
+                )
+            nc.scalar.copy(w_up_all[:, 2 * pair * N : (2 * pair + 2) * N], w_up_psum[:])
 
         negmax = held.tile([PARTS, T], F32, name="negmax")
         nc.vector.tensor_reduce(negmax[:], score[:], AXIS.X, ALU.max, negate=True)
@@ -137,34 +151,23 @@ def tile_clusterlocalatt_kernel(tc, xq, xk, xv, w_qkv, b_qkv, w_up, b_up, base, 
         nc.scalar.copy(attT[:], attT_psum[:])
 
         pooled_v = max_over_positions(nc, held, maps_v, "pooled_v")
-        vT_psum = psum.tile([PARTS, T, H * PARTS], F32, name="vT_psum")
+        vT_psum = psum.tile([PARTS, T, H, PARTS], F32, name="vT_psum")
         for t in range(T):
             for h in range(H):
-                nc.tensor.transpose(
-                    vT_psum[:, t, h * PARTS : (h + 1) * PARTS], pooled_v[:, h, t * L : (t + 1) * L], ident_f32[:]
-                )
-        vT = held.tile([PARTS, T, H * PARTS], BF16, name="vT")
+                nc.tensor.transpose(vT_psum[:, t, h, :], pooled_v[:, h, t * L : (t + 1) * L], ident_f32[:])
+        vT = held.tile([PARTS, T, H, PARTS], BF16, name="vT")
         for t in range(T):
             nc.scalar.activation(
-                vT[:, t, :], vT_psum[:, t, :], ACT.Identity, bias=cols[:, T + t : T + t + 1], scale=cols[:, t : t + 1]
+                vT[:, t], vT_psum[:, t], ACT.Identity, bias=v_cols[:, T + t : T + t + 1], scale=v_cols[:, t : t + 1]
             )
 
-        oT = psum.tile([PARTS, T, H * PARTS], F32, name="oT")
-        for t in range(T):
-            nc.tensor.matmul(oT[:, t, :], attT[:, t, :], vT[:, t, :], start=True, stop=True)
-
-        for a in range(A):
-            scaledT = ring.tile([PARTS, T, H * PARTS], F32, name="scaledT")
+        o = psum.tile([PARTS, H, N], F32, name="o")
+        for h in range(H):
             for t in range(T):
-                w_up_col = cols[:, 2 * T + a * T + t : 2 * T + a * T + t + 1]
-                nc.scalar.mul(scaledT[:, t, :], oT[:, t, :], w_up_col)
-            for h in range(H):
-                flipped = banks.tile([PARTS, BANK], F32, name="flipped", tag="bank")
-                for t in range(T):
-                    nc.tensor.transpose(
-                        flipped[:, t * L : (t + 1) * L], scaledT[:, t, h * PARTS : (h + 1) * PARTS], ident_f32[:]
-                    )
+                nc.tensor.matmul(o[:, h, t * L : (t + 1) * L], vT[:, t, h, :], attT[:, t, :], start=True, stop=True)
+        for h in range(H):
+            for a in range(A):
                 product = ring.tile([PARTS, N], F32, name="product")
-                nc.scalar.copy(product[:], flipped[:, 0:N])
+                nc.vector.tensor_tensor(product[:], o[:, h, :], w_up_all[:, a * N : (a + 1) * N], ALU.mult)
                 nc.vector.tensor_tensor(windows[a, h][:].indirect(offsets[:]), product[:], b_up_all[:], ALU.add)
-                nc.sync.dma_start(out_blocks[a, h], windows[a, h][:])
+                queues[a % 2].dma_start(out_blocks[a, h], windows[a, h][:])

@@ -52,18 +52,14 @@ def tile_clusterlocalatt_kernel(tc, xq, xk, xv, w_qkv, b_qkv, w_up, b_up, base, 
     nc = tc.nc
     with (
         tc.tile_pool(name="held", bufs=1) as held,
-        tc.tile_pool(name="ring", bufs=2) as ring,
         tc.psum_pool(name="psum", bufs=1) as psum,
-        tc.psum_pool(name="banks", bufs=2) as banks,
     ):
         offsets = held.tile([PARTS, N // 16], U16, name="offsets")
         nc.sync.dma_start(offsets[:], offs)
 
-        params = held.tile([1, 11 * N], F32, name="params")
+        params = held.tile([1, 6 * N], F32, name="params")
         nc.scalar.dma_start(params[:, 0 : 3 * N], w_qkv.rearrange("(o r) n -> o (r n)", o=1))
         nc.scalar.dma_start(params[:, 3 * N : 6 * N], b_qkv.rearrange("(o r) n -> o (r n)", o=1))
-        nc.sync.dma_start(params[:, 6 * N : 10 * N], w_up.rearrange("(o a) n -> o (a n)", o=1))
-        nc.sync.dma_start(params[:, 10 * N : 11 * N], b_up)
 
         ones = held.tile([1, PARTS], F32, name="ones")
         nc.gpsimd.memset(ones[:], 1.0)
@@ -79,18 +75,21 @@ def tile_clusterlocalatt_kernel(tc, xq, xk, xv, w_qkv, b_qkv, w_up, b_up, base, 
         maps_q = load_maps(nc, held, xq, "xq")
         maps_k = load_maps(nc, held, xk, "xk")
         maps_v = load_maps(nc, held, xv, "xv")
+        w_up_all = held.tile([PARTS, A * N], F32, name="w_up_all")
+        nc.sync.dma_start(w_up_all[:], w_up.rearrange("a n -> (a n)").partition_broadcast(PARTS))
+        b_up_all = held.tile([PARTS, N], F32, name="b_up_all")
+        nc.sync.dma_start(b_up_all[:], b_up.rearrange("o n -> (o n)").partition_broadcast(PARTS))
         base_blocks = base.rearrange("(a p h) s -> a h p s", a=A, h=H)
         out_blocks = out.rearrange("(a p h) s -> a h p s", a=A, h=H)
-        queues = (nc.sync, nc.scalar)
         windows = {}
         for h in range(H):
             for a in range(A):
                 windows[a, h] = held.tile([PARTS, S], F32, name=f"window{a}{h}")
-                queues[a % 2].dma_start(windows[a, h][:], base_blocks[a, h])
+                nc.sync.dma_start(windows[a, h][:], base_blocks[a, h])
 
         spread = {}
         for r, label in enumerate(("q", "k")):
-            spread[label] = banks.tile([PARTS, 2 * N], F32, name=f"spread_{label}", tag="bank")
+            spread[label] = psum.tile([PARTS, 2 * N], F32, name=f"spread_{label}")
             nc.tensor.matmul(spread[label][:, 0:N], ones[:], params[:, r * N : (r + 1) * N], start=True, stop=True)
             nc.tensor.matmul(
                 spread[label][:, N : 2 * N], ones[:], params[:, (3 + r) * N : (4 + r) * N], start=True, stop=True
@@ -103,10 +102,6 @@ def tile_clusterlocalatt_kernel(tc, xq, xk, xv, w_qkv, b_qkv, w_up, b_up, base, 
             nc.tensor.matmul(v_cols_psum[:, T + t : T + t + 1], bias_row, ones[:, 0:1], start=True, stop=True)
         v_cols = held.tile([PARTS, 2 * T], F32, name="v_cols")
         nc.scalar.copy(v_cols[:], v_cols_psum[:])
-        b_up_psum = psum.tile([PARTS, N], F32, name="b_up_psum")
-        nc.tensor.matmul(b_up_psum[:], ones[:], params[:, 10 * N : 11 * N], start=True, stop=True)
-        b_up_all = held.tile([PARTS, N], F32, name="b_up_all")
-        nc.scalar.copy(b_up_all[:], b_up_psum[:])
 
         q = gain_bias_rounded(nc, held, max_over_positions(nc, held, maps_q, "pooled_q"), spread["q"], "q")
         k = gain_bias_rounded(nc, held, max_over_positions(nc, held, maps_k, "pooled_k"), spread["k"], "k")
@@ -118,17 +113,6 @@ def tile_clusterlocalatt_kernel(tc, xq, xk, xv, w_qkv, b_qkv, w_up, b_up, base, 
                 nc.tensor.matmul(
                     score[:, t, :], q[:, h, cluster], k[:, h, cluster], start=(h == 0), stop=(h == H - 1)
                 )
-
-        w_up_all = held.tile([PARTS, A * N], F32, name="w_up_all")
-        for pair in range(A // 2):
-            w_up_psum = banks.tile([PARTS, 2 * N], F32, name="w_up_psum", tag="bank")
-            for half in range(2):
-                a = 2 * pair + half
-                nc.tensor.matmul(
-                    w_up_psum[:, half * N : (half + 1) * N], ones[:], params[:, (6 + a) * N : (7 + a) * N],
-                    start=True, stop=True,
-                )
-            nc.scalar.copy(w_up_all[:, 2 * pair * N : (2 * pair + 2) * N], w_up_psum[:])
 
         negmax = held.tile([PARTS, T], F32, name="negmax")
         nc.vector.tensor_reduce(negmax[:], score[:], AXIS.X, ALU.max, negate=True)
@@ -165,9 +149,18 @@ def tile_clusterlocalatt_kernel(tc, xq, xk, xv, w_qkv, b_qkv, w_up, b_up, base, 
         for h in range(H):
             for t in range(T):
                 nc.tensor.matmul(o[:, h, t * L : (t + 1) * L], vT[:, t, h, :], attT[:, t, :], start=True, stop=True)
+
+        products = held.tile([PARTS, H, A, N], F32, name="products")
+        nc.vector.tensor_tensor(
+            products[:],
+            o[:].unsqueeze(2).to_broadcast([PARTS, H, A, N]),
+            w_up_all[:].rearrange("p (a n) -> p a n", a=A).unsqueeze(1).to_broadcast([PARTS, H, A, N]),
+            ALU.mult,
+        )
+
         for h in range(H):
             for a in range(A):
-                product = ring.tile([PARTS, N], F32, name="product")
-                nc.vector.tensor_tensor(product[:], o[:, h, :], w_up_all[:, a * N : (a + 1) * N], ALU.mult)
-                nc.vector.tensor_tensor(windows[a, h][:].indirect(offsets[:]), product[:], b_up_all[:], ALU.add)
-                queues[a % 2].dma_start(out_blocks[a, h], windows[a, h][:])
+                nc.vector.tensor_tensor(
+                    windows[a, h][:].indirect(offsets[:]), products[:, h, a, :], b_up_all[:], ALU.add
+                )
+                nc.sync.dma_start(out_blocks[a, h], windows[a, h][:])

@@ -1,5 +1,4 @@
 import concourse.mybir as mybir
-from concourse.masks import make_identity
 
 F32 = mybir.dt.float32
 BF16 = mybir.dt.bfloat16
@@ -52,6 +51,7 @@ def tile_clusterlocalatt_kernel(tc, xq, xk, xv, w_qkv, b_qkv, w_up, b_up, base, 
     nc = tc.nc
     with (
         tc.tile_pool(name="held", bufs=1) as held,
+        tc.tile_pool(name="ring", bufs=2) as ring,
         tc.psum_pool(name="psum", bufs=1) as psum,
     ):
         offsets = held.tile([PARTS, N // 16], U16, name="offsets")
@@ -62,15 +62,23 @@ def tile_clusterlocalatt_kernel(tc, xq, xk, xv, w_qkv, b_qkv, w_up, b_up, base, 
         nc.scalar.dma_start(params[:, 3 * N : 6 * N], b_qkv.rearrange("(o r) n -> o (r n)", o=1))
 
         ones = held.tile([1, PARTS], F32, name="ones")
-        nc.gpsimd.memset(ones[:], 1.0)
-        ident_f32 = held.tile([PARTS, PARTS], F32, name="ident_f32")
-        make_identity(nc, ident_f32[:])
-        ident_bf16 = held.tile([PARTS, PARTS], BF16, name="ident_bf16")
-        make_identity(nc, ident_bf16[:])
+        nc.vector.memset(ones[:], 1.0)
 
         warm = held.tile([PARTS, 1], F32, name="warm")
-        nc.gpsimd.memset(warm[:], 0.0)
+        nc.vector.memset(warm[:], 0.0)
         nc.scalar.activation(warm[:], warm[:], ACT.Exp)
+
+        count = held.tile([1, PARTS], F32, name="count")
+        nc.vector.memset(count[:, 0:1], 0.0)
+        for width in (1, 2, 4, 8, 16, 32, 64):
+            nc.vector.tensor_scalar_add(count[:, width : 2 * width], count[:, 0:width], float(width))
+        count_psum = psum.tile([PARTS, PARTS + 1], F32, name="count_psum")
+        nc.tensor.matmul(count_psum[:, 0:PARTS], ones[:], count[:], start=True, stop=True)
+        nc.tensor.matmul(count_psum[:, PARTS : PARTS + 1], count[:], ones[:, 0:1], start=True, stop=True)
+        ident = held.tile([PARTS, PARTS], F32, name="ident")
+        nc.vector.tensor_scalar(
+            ident[:], count_psum[:, 0:PARTS], count_psum[:, PARTS : PARTS + 1], None, ALU.is_equal
+        )
 
         maps_q = load_maps(nc, held, xq, "xq")
         maps_k = load_maps(nc, held, xk, "xk")
@@ -78,14 +86,15 @@ def tile_clusterlocalatt_kernel(tc, xq, xk, xv, w_qkv, b_qkv, w_up, b_up, base, 
         w_up_all = held.tile([PARTS, A * N], F32, name="w_up_all")
         nc.sync.dma_start(w_up_all[:], w_up.rearrange("a n -> (a n)").partition_broadcast(PARTS))
         b_up_all = held.tile([PARTS, N], F32, name="b_up_all")
-        nc.sync.dma_start(b_up_all[:], b_up.rearrange("o n -> (o n)").partition_broadcast(PARTS))
+        nc.scalar.dma_start(b_up_all[:], b_up.rearrange("o n -> (o n)").partition_broadcast(PARTS))
         base_blocks = base.rearrange("(a p h) s -> a h p s", a=A, h=H)
         out_blocks = out.rearrange("(a p h) s -> a h p s", a=A, h=H)
+        queues = (nc.sync, nc.scalar)
         windows = {}
         for h in range(H):
             for a in range(A):
                 windows[a, h] = held.tile([PARTS, S], F32, name=f"window{a}{h}")
-                nc.sync.dma_start(windows[a, h][:], base_blocks[a, h])
+                queues[a % 2].dma_start(windows[a, h][:], base_blocks[a, h])
 
         spread = {}
         for r, label in enumerate(("q", "k")):
@@ -124,13 +133,13 @@ def tile_clusterlocalatt_kernel(tc, xq, xk, xv, w_qkv, b_qkv, w_up, b_up, base, 
             )
         rsum = held.tile([PARTS, T], F32, name="rsum")
         nc.vector.reciprocal(rsum[:], esum[:])
-        att = held.tile([PARTS, T, L], BF16, name="att")
+        att = held.tile([PARTS, T, L], F32, name="att")
         for t in range(T):
             nc.scalar.mul(att[:, t, :], e[:, t, :], rsum[:, t : t + 1])
 
-        attT_psum = psum.tile([PARTS, T, L], BF16, name="attT_psum")
+        attT_psum = psum.tile([PARTS, T, L], F32, name="attT_psum")
         for t in range(T):
-            nc.tensor.transpose(attT_psum[:, t, :], att[:, t, :], ident_bf16[:])
+            nc.tensor.transpose(attT_psum[:, t, :], att[:, t, :], ident[:])
         attT = held.tile([PARTS, T, L], BF16, name="attT")
         nc.scalar.copy(attT[:], attT_psum[:])
 
@@ -138,7 +147,7 @@ def tile_clusterlocalatt_kernel(tc, xq, xk, xv, w_qkv, b_qkv, w_up, b_up, base, 
         vT_psum = psum.tile([PARTS, T, H, PARTS], F32, name="vT_psum")
         for t in range(T):
             for h in range(H):
-                nc.tensor.transpose(vT_psum[:, t, h, :], pooled_v[:, h, t * L : (t + 1) * L], ident_f32[:])
+                nc.tensor.transpose(vT_psum[:, t, h, :], pooled_v[:, h, t * L : (t + 1) * L], ident[:])
         vT = held.tile([PARTS, T, H, PARTS], BF16, name="vT")
         for t in range(T):
             nc.scalar.activation(
@@ -149,18 +158,9 @@ def tile_clusterlocalatt_kernel(tc, xq, xk, xv, w_qkv, b_qkv, w_up, b_up, base, 
         for h in range(H):
             for t in range(T):
                 nc.tensor.matmul(o[:, h, t * L : (t + 1) * L], vT[:, t, h, :], attT[:, t, :], start=True, stop=True)
-
-        products = held.tile([PARTS, H, A, N], F32, name="products")
-        nc.vector.tensor_tensor(
-            products[:],
-            o[:].unsqueeze(2).to_broadcast([PARTS, H, A, N]),
-            w_up_all[:].rearrange("p (a n) -> p a n", a=A).unsqueeze(1).to_broadcast([PARTS, H, A, N]),
-            ALU.mult,
-        )
-
         for h in range(H):
             for a in range(A):
-                nc.vector.tensor_tensor(
-                    windows[a, h][:].indirect(offsets[:]), products[:, h, a, :], b_up_all[:], ALU.add
-                )
-                nc.sync.dma_start(out_blocks[a, h], windows[a, h][:])
+                product = ring.tile([PARTS, N], F32, name="product")
+                nc.vector.tensor_tensor(product[:], o[:, h, :], w_up_all[:, a * N : (a + 1) * N], ALU.mult)
+                nc.vector.tensor_tensor(windows[a, h][:].indirect(offsets[:]), product[:], b_up_all[:], ALU.add)
+                queues[a % 2].dma_start(out_blocks[a, h], windows[a, h][:])

@@ -1,4 +1,5 @@
 import concourse.mybir as mybir
+from concourse.masks import make_identity
 
 F32 = mybir.dt.float32
 BF16 = mybir.dt.bfloat16
@@ -19,29 +20,29 @@ FLOPS = 2 * (2 * T * L * L * PARTS * H)
 
 
 def load_maps(nc, pool, x, label):
-    by_position = x.rearrange("(a p h) n -> p a (h n)", a=A, h=H)
-    halves = []
-    for half, queue in enumerate((nc.sync, nc.scalar)):
-        two = pool.tile([PARTS, A // 2, H * N], F32, name=f"{label}{half}")
-        queue.dma_start(two[:], by_position[:, half * (A // 2) : (half + 1) * (A // 2), :])
-        halves.append(two)
-    return halves
+    queues = (nc.sync, nc.scalar)
+    maps = []
+    for a in range(A):
+        rows = x[a * H * PARTS : (a + 1) * H * PARTS, :]
+        one = pool.tile([PARTS, H, N], F32, name=f"{label}{a}")
+        queues[a % 2].dma_start(one[:], rows.rearrange("(p h) n -> p h n", h=H))
+        maps.append(one)
+    return maps
 
 
-def max_over_positions(nc, pool, halves, label):
-    pooled = pool.tile([PARTS, H * N], F32, name=label)
-    other = pool.tile([PARTS, H * N], F32, name=f"{label}_other")
-    nc.vector.tensor_max(pooled[:], halves[0][:, 0, :], halves[0][:, 1, :])
-    nc.vector.tensor_max(other[:], halves[1][:, 0, :], halves[1][:, 1, :])
-    nc.vector.tensor_max(pooled[:], pooled[:], other[:])
-    return pooled.rearrange("p (h n) -> p h n", h=H)
+def max_over_positions(nc, pool, maps, label):
+    pooled = pool.tile([PARTS, H, N], F32, name=label)
+    nc.vector.tensor_max(pooled[:], maps[0][:], maps[1][:])
+    for one in maps[2:]:
+        nc.vector.tensor_max(pooled[:], pooled[:], one[:])
+    return pooled
 
 
 def gain_bias_rounded(nc, pool, pooled, spread, label):
     gain = spread[:, 0:N].unsqueeze(1).to_broadcast([PARTS, H, N])
     bias = spread[:, N : 2 * N].unsqueeze(1).to_broadcast([PARTS, H, N])
     scaled = pool.tile([PARTS, H, N], F32, name=f"{label}_scaled")
-    nc.vector.tensor_tensor(scaled[:], pooled, gain, ALU.mult)
+    nc.vector.tensor_tensor(scaled[:], pooled[:], gain, ALU.mult)
     rounded = pool.tile([PARTS, H, N], BF16, name=label)
     nc.vector.tensor_tensor(rounded[:], scaled[:], bias, ALU.add)
     return rounded
@@ -53,6 +54,7 @@ def tile_clusterlocalatt_kernel(tc, xq, xk, xv, w_qkv, b_qkv, w_up, b_up, base, 
         tc.tile_pool(name="held", bufs=1) as held,
         tc.tile_pool(name="ring", bufs=2) as ring,
         tc.psum_pool(name="psum", bufs=1) as psum,
+        tc.psum_pool(name="banks", bufs=2) as banks,
     ):
         offsets = held.tile([PARTS, N // 16], U16, name="offsets")
         nc.sync.dma_start(offsets[:], offs)
@@ -62,23 +64,15 @@ def tile_clusterlocalatt_kernel(tc, xq, xk, xv, w_qkv, b_qkv, w_up, b_up, base, 
         nc.scalar.dma_start(params[:, 3 * N : 6 * N], b_qkv.rearrange("(o r) n -> o (r n)", o=1))
 
         ones = held.tile([1, PARTS], F32, name="ones")
-        nc.vector.memset(ones[:], 1.0)
+        nc.gpsimd.memset(ones[:], 1.0)
+        ident_f32 = held.tile([PARTS, PARTS], F32, name="ident_f32")
+        make_identity(nc, ident_f32[:])
+        ident_bf16 = held.tile([PARTS, PARTS], BF16, name="ident_bf16")
+        make_identity(nc, ident_bf16[:])
 
         warm = held.tile([PARTS, 1], F32, name="warm")
-        nc.vector.memset(warm[:], 0.0)
+        nc.gpsimd.memset(warm[:], 0.0)
         nc.scalar.activation(warm[:], warm[:], ACT.Exp)
-
-        count = held.tile([1, PARTS], F32, name="count")
-        nc.vector.memset(count[:, 0:1], 0.0)
-        for width in (1, 2, 4, 8, 16, 32, 64):
-            nc.vector.tensor_scalar_add(count[:, width : 2 * width], count[:, 0:width], float(width))
-        count_psum = psum.tile([PARTS, PARTS + 1], F32, name="count_psum")
-        nc.tensor.matmul(count_psum[:, 0:PARTS], ones[:], count[:], start=True, stop=True)
-        nc.tensor.matmul(count_psum[:, PARTS : PARTS + 1], count[:], ones[:, 0:1], start=True, stop=True)
-        ident = held.tile([PARTS, PARTS], F32, name="ident")
-        nc.vector.tensor_scalar(
-            ident[:], count_psum[:, 0:PARTS], count_psum[:, PARTS : PARTS + 1], None, ALU.is_equal
-        )
 
         maps_q = load_maps(nc, held, xq, "xq")
         maps_k = load_maps(nc, held, xk, "xk")
@@ -86,19 +80,18 @@ def tile_clusterlocalatt_kernel(tc, xq, xk, xv, w_qkv, b_qkv, w_up, b_up, base, 
         w_up_all = held.tile([PARTS, A * N], F32, name="w_up_all")
         nc.sync.dma_start(w_up_all[:], w_up.rearrange("a n -> (a n)").partition_broadcast(PARTS))
         b_up_all = held.tile([PARTS, N], F32, name="b_up_all")
-        nc.scalar.dma_start(b_up_all[:], b_up.rearrange("o n -> (o n)").partition_broadcast(PARTS))
+        nc.sync.dma_start(b_up_all[:], b_up.rearrange("o n -> (o n)").partition_broadcast(PARTS))
         base_blocks = base.rearrange("(a p h) s -> a h p s", a=A, h=H)
         out_blocks = out.rearrange("(a p h) s -> a h p s", a=A, h=H)
-        queues = (nc.sync, nc.scalar)
         windows = {}
         for h in range(H):
             for a in range(A):
                 windows[a, h] = held.tile([PARTS, S], F32, name=f"window{a}{h}")
-                queues[a % 2].dma_start(windows[a, h][:], base_blocks[a, h])
+                nc.sync.dma_start(windows[a, h][:], base_blocks[a, h])
 
         spread = {}
         for r, label in enumerate(("q", "k")):
-            spread[label] = psum.tile([PARTS, 2 * N], F32, name=f"spread_{label}")
+            spread[label] = banks.tile([PARTS, 2 * N], F32, name=f"spread_{label}", tag="bank")
             nc.tensor.matmul(spread[label][:, 0:N], ones[:], params[:, r * N : (r + 1) * N], start=True, stop=True)
             nc.tensor.matmul(
                 spread[label][:, N : 2 * N], ones[:], params[:, (3 + r) * N : (4 + r) * N], start=True, stop=True
@@ -115,52 +108,48 @@ def tile_clusterlocalatt_kernel(tc, xq, xk, xv, w_qkv, b_qkv, w_up, b_up, base, 
         q = gain_bias_rounded(nc, held, max_over_positions(nc, held, maps_q, "pooled_q"), spread["q"], "q")
         k = gain_bias_rounded(nc, held, max_over_positions(nc, held, maps_k, "pooled_k"), spread["k"], "k")
 
-        score = psum.tile([PARTS, T, L], F32, name="score")
+        attT = []
         for t in range(T):
             cluster = slice(t * L, (t + 1) * L)
+            score = psum.tile([PARTS, L], F32, name=f"score{t}")
             for h in range(H):
-                nc.tensor.matmul(
-                    score[:, t, :], q[:, h, cluster], k[:, h, cluster], start=(h == 0), stop=(h == H - 1)
-                )
+                nc.tensor.matmul(score[:], q[:, h, cluster], k[:, h, cluster], start=(h == 0), stop=(h == H - 1))
+            negmax = held.tile([PARTS, 1], F32, name=f"negmax{t}")
+            nc.vector.tensor_reduce(negmax[:], score[:], AXIS.X, ALU.max, negate=True)
+            e = held.tile([PARTS, L], F32, name=f"e{t}")
+            esum = held.tile([PARTS, 1], F32, name=f"esum{t}")
+            nc.scalar.activation(e[:], score[:], ACT.Exp, bias=negmax[:], scale=1.0, accum_out=esum[:])
+            rsum = held.tile([PARTS, 1], F32, name=f"rsum{t}")
+            nc.vector.reciprocal(rsum[:], esum[:])
+            att = held.tile([PARTS, L], BF16, name=f"att{t}")
+            nc.scalar.mul(att[:], e[:], rsum[:])
+            attT_psum = banks.tile([PARTS, L], BF16, name=f"attT_psum{t}", tag="bank")
+            nc.tensor.transpose(attT_psum[:], att[:], ident_bf16[:])
+            attT.append(held.tile([PARTS, L], BF16, name=f"attT{t}"))
+            nc.scalar.copy(attT[t][:], attT_psum[:])
 
-        negmax = held.tile([PARTS, T], F32, name="negmax")
-        nc.vector.tensor_reduce(negmax[:], score[:], AXIS.X, ALU.max, negate=True)
-        e = held.tile([PARTS, T, L], F32, name="e")
-        esum = held.tile([PARTS, T], F32, name="esum")
+        vT = []
         for t in range(T):
-            nc.scalar.activation(
-                e[:, t, :], score[:, t, :], ACT.Exp, bias=negmax[:, t : t + 1], scale=1.0, accum_out=esum[:, t : t + 1]
-            )
-        rsum = held.tile([PARTS, T], F32, name="rsum")
-        nc.vector.reciprocal(rsum[:], esum[:])
-        att = held.tile([PARTS, T, L], F32, name="att")
-        for t in range(T):
-            nc.scalar.mul(att[:, t, :], e[:, t, :], rsum[:, t : t + 1])
-
-        attT_psum = psum.tile([PARTS, T, L], F32, name="attT_psum")
-        for t in range(T):
-            nc.tensor.transpose(attT_psum[:, t, :], att[:, t, :], ident[:])
-        attT = held.tile([PARTS, T, L], BF16, name="attT")
-        nc.scalar.copy(attT[:], attT_psum[:])
-
-        pooled_v = max_over_positions(nc, held, maps_v, "pooled_v")
-        vT_psum = psum.tile([PARTS, T, H, PARTS], F32, name="vT_psum")
-        for t in range(T):
+            cluster = slice(t * L, (t + 1) * L)
+            pooled_v = held.tile([PARTS, H, L], F32, name=f"pooled_v{t}")
+            nc.vector.tensor_max(pooled_v[:], maps_v[0][:, :, cluster], maps_v[1][:, :, cluster])
+            for one in maps_v[2:]:
+                nc.vector.tensor_max(pooled_v[:], pooled_v[:], one[:, :, cluster])
+            vT_psum = psum.tile([PARTS, H, PARTS], F32, name=f"vT_psum{t}")
             for h in range(H):
-                nc.tensor.transpose(vT_psum[:, t, h, :], pooled_v[:, h, t * L : (t + 1) * L], ident[:])
-        vT = held.tile([PARTS, T, H, PARTS], BF16, name="vT")
-        for t in range(T):
+                nc.tensor.transpose(vT_psum[:, h, :], pooled_v[:, h, :], ident_f32[:])
+            vT.append(held.tile([PARTS, H, PARTS], BF16, name=f"vT{t}"))
             nc.scalar.activation(
-                vT[:, t], vT_psum[:, t], ACT.Identity, bias=v_cols[:, T + t : T + t + 1], scale=v_cols[:, t : t + 1]
+                vT[t][:], vT_psum[:], ACT.Identity, bias=v_cols[:, T + t : T + t + 1], scale=v_cols[:, t : t + 1]
             )
 
         o = psum.tile([PARTS, H, N], F32, name="o")
-        for h in range(H):
-            for t in range(T):
-                nc.tensor.matmul(o[:, h, t * L : (t + 1) * L], vT[:, t, h, :], attT[:, t, :], start=True, stop=True)
+        for t in range(T):
+            for h in range(H):
+                nc.tensor.matmul(o[:, h, t * L : (t + 1) * L], vT[t][:, h, :], attT[t][:], start=True, stop=True)
         for h in range(H):
             for a in range(A):
                 product = ring.tile([PARTS, N], F32, name="product")
                 nc.vector.tensor_tensor(product[:], o[:, h, :], w_up_all[:, a * N : (a + 1) * N], ALU.mult)
                 nc.vector.tensor_tensor(windows[a, h][:].indirect(offsets[:]), product[:], b_up_all[:], ALU.add)
-                queues[a % 2].dma_start(out_blocks[a, h], windows[a, h][:])
+                nc.sync.dma_start(out_blocks[a, h], windows[a, h][:])

@@ -122,34 +122,36 @@ def tile_clusterlocalatt_kernel(tc, xq, xk, xv, w_qkv, b_qkv, w_up, b_up, base, 
             rsum = held.tile([PARTS, 1], F32, name=f"rsum{t}")
             nc.vector.reciprocal(rsum[:], esum[:])
             att = held.tile([PARTS, L], BF16, name=f"att{t}")
-            nc.scalar.mul(att[:], e[:], rsum[:])
+            nc.vector.tensor_scalar_mul(att[:], e[:], rsum[:])
             attT_psum = banks.tile([PARTS, L], BF16, name=f"attT_psum{t}", tag="bank")
             nc.tensor.transpose(attT_psum[:], att[:], ident_bf16[:])
             attT.append(held.tile([PARTS, L], BF16, name=f"attT{t}"))
-            nc.scalar.copy(attT[t][:], attT_psum[:])
+            nc.vector.tensor_copy(attT[t][:], attT_psum[:])
 
         vT = []
-        for t in range(T):
-            cluster = slice(t * L, (t + 1) * L)
-            pooled_v = held.tile([PARTS, H, L], F32, name=f"pooled_v{t}")
-            nc.vector.tensor_max(pooled_v[:], maps_v[0][:, :, cluster], maps_v[1][:, :, cluster])
-            for one in maps_v[2:]:
-                nc.vector.tensor_max(pooled_v[:], pooled_v[:], one[:, :, cluster])
-            vT_psum = psum.tile([PARTS, H, PARTS], F32, name=f"vT_psum{t}")
-            for h in range(H):
-                nc.tensor.transpose(vT_psum[:, h, :], pooled_v[:, h, :], ident_f32[:])
-            vT.append(held.tile([PARTS, H, PARTS], BF16, name=f"vT{t}"))
-            nc.scalar.activation(
-                vT[t][:], vT_psum[:], ACT.Identity, bias=v_cols[:, T + t : T + t + 1], scale=v_cols[:, t : t + 1]
-            )
-
-        o = psum.tile([PARTS, H, N], F32, name="o")
-        for t in range(T):
-            for h in range(H):
-                nc.tensor.matmul(o[:, h, t * L : (t + 1) * L], vT[t][:, h, :], attT[t][:], start=True, stop=True)
         for h in range(H):
+            pooled_v = held.tile([PARTS, N], F32, name=f"pooled_v{h}")
+            nc.vector.tensor_max(pooled_v[:], maps_v[0][:, h, :], maps_v[1][:, h, :])
+            for one in maps_v[2:]:
+                nc.vector.tensor_max(pooled_v[:], pooled_v[:], one[:, h, :])
+            vT_psum = psum.tile([PARTS, T, PARTS], F32, name=f"vT_psum{h}")
+            vT.append(held.tile([PARTS, T, PARTS], BF16, name=f"vT{h}"))
+            for t in range(T):
+                nc.tensor.transpose(vT_psum[:, t, :], pooled_v[:, t * L : (t + 1) * L], ident_f32[:])
+                nc.scalar.activation(
+                    vT[h][:, t, :],
+                    vT_psum[:, t, :],
+                    ACT.Identity,
+                    bias=v_cols[:, T + t : T + t + 1],
+                    scale=v_cols[:, t : t + 1],
+                )
+
+        for h in range(H):
+            o = psum.tile([PARTS, N], F32, name=f"o{h}", tag=f"score{h}")
+            for t in range(T):
+                nc.tensor.matmul(o[:, t * L : (t + 1) * L], vT[h][:, t, :], attT[t][:], start=True, stop=True)
             for a in range(A):
                 product = ring.tile([PARTS, N], F32, name="product")
-                nc.vector.tensor_tensor(product[:], o[:, h, :], w_up_all[:, a * N : (a + 1) * N], ALU.mult)
+                nc.vector.tensor_tensor(product[:], o[:], w_up_all[:, a * N : (a + 1) * N], ALU.mult)
                 nc.vector.tensor_tensor(windows[a, h][:].indirect(offsets[:]), product[:], b_up_all[:], ALU.add)
                 nc.sync.dma_start(out_blocks[a, h], windows[a, h][:])

@@ -52,7 +52,7 @@ def tile_clusterlocalatt_kernel(tc, xq, xk, xv, w_qkv, b_qkv, w_up, b_up, base, 
     nc = tc.nc
     with (
         tc.tile_pool(name="held", bufs=1) as held,
-        tc.tile_pool(name="ring", bufs=2) as ring,
+        tc.tile_pool(name="ring", bufs=3) as ring,
         tc.psum_pool(name="psum", bufs=1) as psum,
         tc.psum_pool(name="banks", bufs=2) as banks,
     ):
@@ -146,12 +146,20 @@ def tile_clusterlocalatt_kernel(tc, xq, xk, xv, w_qkv, b_qkv, w_up, b_up, base, 
                     scale=v_cols[:, t : t + 1],
                 )
 
+        o = []
         for h in range(H):
-            o = psum.tile([PARTS, N], F32, name=f"o{h}", tag=f"score{h}")
+            o.append(psum.tile([PARTS, N], F32, name=f"o{h}", tag=f"score{h}"))
             for t in range(T):
-                nc.tensor.matmul(o[:, t * L : (t + 1) * L], vT[h][:, t, :], attT[t][:], start=True, stop=True)
-            for a in range(A):
-                product = ring.tile([PARTS, N], F32, name="product")
-                nc.vector.tensor_tensor(product[:], o[:], w_up_all[:, a * N : (a + 1) * N], ALU.mult)
-                nc.vector.tensor_tensor(windows[a, h][:].indirect(offsets[:]), product[:], b_up_all[:], ALU.add)
+                nc.tensor.matmul(o[h][:, t * L : (t + 1) * L], vT[h][:, t, :], attT[t][:], start=True, stop=True)
+
+        blocks = [(a, h) for h in range(H) for a in range(A)]
+        products = []
+        for n in range(len(blocks) + 1):
+            if n < len(blocks):
+                a, h = blocks[n]
+                products.append(ring.tile([PARTS, N], F32, name="product"))
+                nc.vector.tensor_tensor(products[n][:], o[h][:], w_up_all[:, a * N : (a + 1) * N], ALU.mult)
+            if n > 0:
+                a, h = blocks[n - 1]
+                nc.vector.tensor_tensor(windows[a, h][:].indirect(offsets[:]), products[n - 1][:], b_up_all[:], ALU.add)
                 nc.sync.dma_start(out_blocks[a, h], windows[a, h][:])

@@ -19,10 +19,10 @@ S = 512
 FLOPS = 2 * (2 * T * L * L * PARTS * H)
 
 
-def load_maps(nc, pool, x, label):
+def load_maps(nc, pool, x, label, positions):
     queues = (nc.sync, nc.scalar)
     maps = []
-    for a in range(A):
+    for a in positions:
         rows = x[a * H * PARTS : (a + 1) * H * PARTS, :]
         one = pool.tile([PARTS, H, N], F32, name=f"{label}{a}")
         queues[a % 2].dma_start(one[:], rows.rearrange("(p h) n -> p h n", h=H))
@@ -56,13 +56,6 @@ def tile_clusterlocalatt_kernel(tc, xq, xk, xv, w_qkv, b_qkv, w_up, b_up, base, 
         tc.psum_pool(name="psum", bufs=1) as psum,
         tc.psum_pool(name="banks", bufs=2) as banks,
     ):
-        offsets = held.tile([PARTS, N // 16], U16, name="offsets")
-        nc.sync.dma_start(offsets[:], offs)
-
-        params = held.tile([1, 6 * N], F32, name="params")
-        nc.scalar.dma_start(params[:, 0 : 3 * N], w_qkv.rearrange("(o r) n -> o (r n)", o=1))
-        nc.scalar.dma_start(params[:, 3 * N : 6 * N], b_qkv.rearrange("(o r) n -> o (r n)", o=1))
-
         ones = held.tile([1, PARTS], F32, name="ones")
         nc.gpsimd.memset(ones[:], 1.0)
         ident_f32 = held.tile([PARTS, PARTS], F32, name="ident_f32")
@@ -70,13 +63,15 @@ def tile_clusterlocalatt_kernel(tc, xq, xk, xv, w_qkv, b_qkv, w_up, b_up, base, 
         ident_bf16 = held.tile([PARTS, PARTS], BF16, name="ident_bf16")
         make_identity(nc, ident_bf16[:])
 
-        warm = held.tile([PARTS, 1], F32, name="warm")
-        nc.gpsimd.memset(warm[:], 0.0)
-        nc.scalar.activation(warm[:], warm[:], ACT.Exp)
-
-        maps_q = load_maps(nc, held, xq, "xq")
-        maps_k = load_maps(nc, held, xk, "xk")
-        maps_v = load_maps(nc, held, xv, "xv")
+        maps_q = load_maps(nc, held, xq, "xq", range(0, 2))
+        params = held.tile([1, 6 * N], F32, name="params")
+        nc.sync.dma_start(params[:, 0 : 3 * N], w_qkv.rearrange("(o r) n -> o (r n)", o=1))
+        nc.scalar.dma_start(params[:, 3 * N : 6 * N], b_qkv.rearrange("(o r) n -> o (r n)", o=1))
+        maps_q += load_maps(nc, held, xq, "xq", range(2, A))
+        maps_k = load_maps(nc, held, xk, "xk", range(A))
+        maps_v = load_maps(nc, held, xv, "xv", range(A))
+        offsets = held.tile([PARTS, N // 16], U16, name="offsets")
+        nc.sync.dma_start(offsets[:], offs)
         w_up_all = held.tile([PARTS, A * N], F32, name="w_up_all")
         nc.sync.dma_start(w_up_all[:], w_up.rearrange("a n -> (a n)").partition_broadcast(PARTS))
         b_up_all = held.tile([PARTS, N], F32, name="b_up_all")
@@ -88,6 +83,10 @@ def tile_clusterlocalatt_kernel(tc, xq, xk, xv, w_qkv, b_qkv, w_up, b_up, base, 
             for a in range(A):
                 windows[a, h] = held.tile([PARTS, S], F32, name=f"window{a}{h}")
                 nc.sync.dma_start(windows[a, h][:], base_blocks[a, h])
+
+        warm = held.tile([PARTS, 1], F32, name="warm")
+        nc.gpsimd.memset(warm[:], 0.0)
+        nc.scalar.activation(warm[:], warm[:], ACT.Exp)
 
         spread = {}
         for r, label in enumerate(("q", "k")):

@@ -84,10 +84,6 @@ def tile_clusterlocalatt_kernel(tc, xq, xk, xv, w_qkv, b_qkv, w_up, b_up, base, 
                 windows[a, h] = held.tile([PARTS, S], F32, name=f"window{a}{h}")
                 nc.sync.dma_start(windows[a, h][:], base_blocks[a, h])
 
-        warm = held.tile([PARTS, 1], F32, name="warm")
-        nc.gpsimd.memset(warm[:], 0.0)
-        nc.scalar.activation(warm[:], warm[:], ACT.Exp)
-
         spread = {}
         for r, label in enumerate(("q", "k")):
             spread[label] = banks.tile([PARTS, 2 * N], F32, name=f"spread_{label}", tag="bank")

@@ -52,7 +52,7 @@ def tile_clusterlocalatt_kernel(tc, xq, xk, xv, w_qkv, b_qkv, w_up, b_up, base, 
     nc = tc.nc
     with (
         tc.tile_pool(name="held", bufs=1) as held,
-        tc.tile_pool(name="ring", bufs=3) as ring,
+        tc.tile_pool(name="ring", bufs=2) as ring,
         tc.psum_pool(name="psum", bufs=1) as psum,
         tc.psum_pool(name="banks", bufs=2) as banks,
     ):
@@ -141,20 +141,12 @@ def tile_clusterlocalatt_kernel(tc, xq, xk, xv, w_qkv, b_qkv, w_up, b_up, base, 
                     scale=v_cols[:, t : t + 1],
                 )
 
-        o = []
         for h in range(H):
-            o.append(psum.tile([PARTS, N], F32, name=f"o{h}", tag=f"score{h}"))
+            o = psum.tile([PARTS, N], F32, name=f"o{h}", tag=f"score{h}")
             for t in range(T):
-                nc.tensor.matmul(o[h][:, t * L : (t + 1) * L], vT[h][:, t, :], attT[t][:], start=True, stop=True)
-
-        blocks = [(a, h) for h in range(H) for a in range(A)]
-        products = []
-        for n in range(len(blocks) + 1):
-            if n < len(blocks):
-                a, h = blocks[n]
-                products.append(ring.tile([PARTS, N], F32, name="product"))
-                nc.vector.tensor_tensor(products[n][:], o[h][:], w_up_all[:, a * N : (a + 1) * N], ALU.mult)
-            if n > 0:
-                a, h = blocks[n - 1]
-                nc.vector.tensor_tensor(windows[a, h][:].indirect(offsets[:]), products[n - 1][:], b_up_all[:], ALU.add)
+                nc.tensor.matmul(o[:, t * L : (t + 1) * L], vT[h][:, t, :], attT[t][:], start=True, stop=True)
+            for a in range(A):
+                product = ring.tile([PARTS, N], F32, name="product")
+                nc.vector.tensor_tensor(product[:], o[:], w_up_all[:, a * N : (a + 1) * N], ALU.mult)
+                nc.vector.tensor_tensor(windows[a, h][:].indirect(offsets[:]), product[:], b_up_all[:], ALU.add)
                 nc.sync.dma_start(out_blocks[a, h], windows[a, h][:])

@@ -72,15 +72,17 @@ def tile_clusterlocalatt_kernel(tc, xq, xk, xv, w_qkv, b_qkv, w_up, b_up, base, 
         maps_v = load_maps(nc, held, xv, "xv", range(A))
         offsets = held.tile([PARTS, N // 16], U16, name="offsets")
         nc.sync.dma_start(offsets[:], offs)
-        w_up_all = held.tile([PARTS, A * N], F32, name="w_up_all")
-        nc.sync.dma_start(w_up_all[:], w_up.rearrange("a n -> (a n)").partition_broadcast(PARTS))
+        w_up_first = held.tile([PARTS, N], F32, name="w_up_first")
+        nc.sync.dma_start(w_up_first[:], w_up[0:1, :].rearrange("o n -> (o n)").partition_broadcast(PARTS))
+        w_up_cols = held.tile([PARTS, A * T], F32, name="w_up_cols")
+        nc.scalar.dma_start(w_up_cols[:], w_up.rearrange("a (t p) -> p (a t)", p=PARTS))
         b_up_all = held.tile([PARTS, N], F32, name="b_up_all")
         nc.sync.dma_start(b_up_all[:], b_up.rearrange("o n -> (o n)").partition_broadcast(PARTS))
         base_blocks = base.rearrange("(a p h) s -> a h p s", a=A, h=H)
         out_blocks = out.rearrange("(a p h) s -> a h p s", a=A, h=H)
         windows = {}
-        for h in range(H):
-            for a in range(A):
+        for a in range(A):
+            for h in range(H):
                 windows[a, h] = held.tile([PARTS, S], F32, name=f"window{a}{h}")
                 nc.sync.dma_start(windows[a, h][:], base_blocks[a, h])
 
@@ -141,12 +143,35 @@ def tile_clusterlocalatt_kernel(tc, xq, xk, xv, w_qkv, b_qkv, w_up, b_up, base, 
                     scale=v_cols[:, t : t + 1],
                 )
 
+        o = []
         for h in range(H):
-            o = psum.tile([PARTS, N], F32, name=f"o{h}", tag=f"score{h}")
+            o.append(psum.tile([PARTS, N], F32, name=f"o{h}", tag=f"score{h}"))
             for t in range(T):
-                nc.tensor.matmul(o[:, t * L : (t + 1) * L], vT[h][:, t, :], attT[t][:], start=True, stop=True)
-            for a in range(A):
+                nc.tensor.matmul(o[h][:, t * L : (t + 1) * L], vT[h][:, t, :], attT[t][:], start=True, stop=True)
+        oT = []
+        for t in range(T):
+            oT.append(psum.tile([PARTS, H, PARTS], F32, name=f"oT{t}", tag=f"vT_psum{t}"))
+            for h in range(H):
+                nc.tensor.matmul(oT[t][:, h, :], attT[t][:], vT[h][:, t, :], start=True, stop=True)
+
+        def place(a, h, product):
+            nc.vector.tensor_tensor(windows[a, h][:].indirect(offsets[:]), product[:], b_up_all[:], ALU.add)
+            nc.sync.dma_start(out_blocks[a, h], windows[a, h][:])
+
+        for h in range(H):
+            product = ring.tile([PARTS, N], F32, name="product")
+            nc.vector.tensor_tensor(product[:], o[h][:], w_up_first[:], ALU.mult)
+            place(0, h, product)
+
+        for a in range(1, A):
+            scaledT = []
+            for t in range(T):
+                scaledT.append(ring.tile([PARTS, H, PARTS], F32, name=f"scaledT{t}"))
+                nc.scalar.mul(scaledT[t][:], oT[t][:], w_up_cols[:, a * T + t : a * T + t + 1])
+            for h in range(H):
+                product_psum = banks.tile([PARTS, N], F32, name="product_psum", tag="bank")
+                for t in range(T):
+                    nc.tensor.transpose(product_psum[:, t * L : (t + 1) * L], scaledT[t][:, h, :], ident_f32[:])
                 product = ring.tile([PARTS, N], F32, name="product")
-                nc.vector.tensor_tensor(product[:], o[:], w_up_all[:, a * N : (a + 1) * N], ALU.mult)
-                nc.vector.tensor_tensor(windows[a, h][:].indirect(offsets[:]), product[:], b_up_all[:], ALU.add)
-                nc.sync.dma_start(out_blocks[a, h], windows[a, h][:])
+                nc.scalar.copy(product[:], product_psum[:])
+                place(a, h, product)

@@ -81,8 +81,8 @@ def tile_clusterlocalatt_kernel(tc, xq, xk, xv, w_qkv, b_qkv, w_up, b_up, base, 
         base_blocks = base.rearrange("(a p h) s -> a h p s", a=A, h=H)
         out_blocks = out.rearrange("(a p h) s -> a h p s", a=A, h=H)
         windows = {}
-        for a in range(A):
-            for h in range(H):
+        for h in range(H):
+            for a in range(A):
                 windows[a, h] = held.tile([PARTS, S], F32, name=f"window{a}{h}")
                 nc.sync.dma_start(windows[a, h][:], base_blocks[a, h])
 
@@ -143,35 +143,29 @@ def tile_clusterlocalatt_kernel(tc, xq, xk, xv, w_qkv, b_qkv, w_up, b_up, base, 
                     scale=v_cols[:, t : t + 1],
                 )
 
-        o = []
-        for h in range(H):
-            o.append(psum.tile([PARTS, N], F32, name=f"o{h}", tag=f"score{h}"))
-            for t in range(T):
-                nc.tensor.matmul(o[h][:, t * L : (t + 1) * L], vT[h][:, t, :], attT[t][:], start=True, stop=True)
-        oT = []
-        for t in range(T):
-            oT.append(psum.tile([PARTS, H, PARTS], F32, name=f"oT{t}", tag=f"vT_psum{t}"))
-            for h in range(H):
-                nc.tensor.matmul(oT[t][:, h, :], attT[t][:], vT[h][:, t, :], start=True, stop=True)
-
         def place(a, h, product):
             nc.vector.tensor_tensor(windows[a, h][:].indirect(offsets[:]), product[:], b_up_all[:], ALU.add)
             nc.sync.dma_start(out_blocks[a, h], windows[a, h][:])
 
-        for h in range(H):
-            product = ring.tile([PARTS, N], F32, name="product")
-            nc.vector.tensor_tensor(product[:], o[h][:], w_up_first[:], ALU.mult)
-            place(0, h, product)
+        o = psum.tile([PARTS, N], F32, name="o", tag="score0")
+        for t in range(T):
+            nc.tensor.matmul(o[:, t * L : (t + 1) * L], vT[0][:, t, :], attT[t][:], start=True, stop=True)
+        product = ring.tile([PARTS, N], F32, name="product")
+        nc.vector.tensor_tensor(product[:], o[:], w_up_first[:], ALU.mult)
+        place(0, 0, product)
 
-        for a in range(1, A):
-            scaledT = []
+        for h in range(H):
+            oT = psum.tile([PARTS, T, PARTS], F32, name=f"oT{h}", tag=f"vT_psum{h}")
             for t in range(T):
-                scaledT.append(ring.tile([PARTS, H, PARTS], F32, name=f"scaledT{t}"))
-                nc.scalar.mul(scaledT[t][:], oT[t][:], w_up_cols[:, a * T + t : a * T + t + 1])
-            for h in range(H):
+                nc.tensor.matmul(oT[:, t, :], attT[t][:], vT[h][:, t, :], start=True, stop=True)
+            for a in range(A):
+                if (a, h) == (0, 0):
+                    continue
                 product_psum = banks.tile([PARTS, N], F32, name="product_psum", tag="bank")
                 for t in range(T):
-                    nc.tensor.transpose(product_psum[:, t * L : (t + 1) * L], scaledT[t][:, h, :], ident_f32[:])
+                    scaledT = ring.tile([PARTS, PARTS], F32, name=f"scaledT{t}")
+                    nc.scalar.mul(scaledT[:], oT[:, t, :], w_up_cols[:, a * T + t : a * T + t + 1])
+                    nc.tensor.transpose(product_psum[:, t * L : (t + 1) * L], scaledT[:], ident_f32[:])
                 product = ring.tile([PARTS, N], F32, name="product")
                 nc.scalar.copy(product[:], product_psum[:])
                 place(a, h, product)

@@ -147,11 +147,12 @@ def tile_clusterlocalatt_kernel(tc, xq, xk, xv, w_qkv, b_qkv, w_up, b_up, base, 
             nc.vector.tensor_tensor(windows[a, h][:].indirect(offsets[:]), product[:], b_up_all[:], ALU.add)
             nc.sync.dma_start(out_blocks[a, h], windows[a, h][:])
 
-        o = psum.tile([PARTS, N], F32, name="o", tag="score0")
-        for t in range(T):
-            nc.tensor.matmul(o[:, t * L : (t + 1) * L], vT[0][:, t, :], attT[t][:], start=True, stop=True)
         product = ring.tile([PARTS, N], F32, name="product")
-        nc.vector.tensor_tensor(product[:], o[:], w_up_first[:], ALU.mult)
+        for t in range(T):
+            cluster = slice(t * L, (t + 1) * L)
+            o = psum.tile([PARTS, L], F32, name=f"o{t}", tag=f"score{t}")
+            nc.tensor.matmul(o[:], vT[0][:, t, :], attT[t][:], start=True, stop=True)
+            nc.vector.tensor_tensor(product[:, cluster], o[:], w_up_first[:, cluster], ALU.mult)
         place(0, 0, product)
 
         for h in range(H):

import concourse.mybir as mybir
from concourse.masks import make_identity

F32 = mybir.dt.float32
BF16 = mybir.dt.bfloat16
U16 = mybir.dt.uint16
ALU = mybir.AluOpType
ACT = mybir.ActivationFunctionType
AXIS = mybir.AxisListType

PARTS = 128
A = 4
H = 2
N = 256
T = 2
L = 128
S = 512

FLOPS = 2 * (2 * T * L * L * PARTS * H)


def load_maps(nc, pool, x, label, positions):
    queues = (nc.sync, nc.scalar)
    maps = []
    for a in positions:
        rows = x[a * H * PARTS : (a + 1) * H * PARTS, :]
        one = pool.tile([PARTS, H, N], F32, name=f"{label}{a}")
        queues[a % 2].dma_start(one[:], rows.rearrange("(p h) n -> p h n", h=H))
        maps.append(one)
    return maps


def max_over_positions(nc, pool, maps, label):
    pooled = pool.tile([PARTS, H, N], F32, name=label)
    nc.vector.tensor_max(pooled[:], maps[0][:], maps[1][:])
    for one in maps[2:]:
        nc.vector.tensor_max(pooled[:], pooled[:], one[:])
    return pooled


def gain_bias_rounded(nc, pool, pooled, spread, label):
    gain = spread[:, 0:N].unsqueeze(1).to_broadcast([PARTS, H, N])
    bias = spread[:, N : 2 * N].unsqueeze(1).to_broadcast([PARTS, H, N])
    scaled = pool.tile([PARTS, H, N], F32, name=f"{label}_scaled")
    nc.vector.tensor_tensor(scaled[:], pooled[:], gain, ALU.mult)
    rounded = pool.tile([PARTS, H, N], BF16, name=label)
    nc.vector.tensor_tensor(rounded[:], scaled[:], bias, ALU.add)
    return rounded


def tile_clusterlocalatt_kernel(tc, xq, xk, xv, w_qkv, b_qkv, w_up, b_up, base, offs, out):
    nc = tc.nc
    with (
        tc.tile_pool(name="held", bufs=1) as held,
        tc.tile_pool(name="ring", bufs=2) as ring,
        tc.psum_pool(name="psum", bufs=1) as psum,
        tc.psum_pool(name="banks", bufs=2) as banks,
    ):
        ones = held.tile([1, PARTS], F32, name="ones")
        nc.gpsimd.memset(ones[:], 1.0)
        ident_f32 = held.tile([PARTS, PARTS], F32, name="ident_f32")
        make_identity(nc, ident_f32[:])
        ident_bf16 = held.tile([PARTS, PARTS], BF16, name="ident_bf16")
        make_identity(nc, ident_bf16[:])

        maps_q = load_maps(nc, held, xq, "xq", range(0, 2))
        params = held.tile([1, 6 * N], F32, name="params")
        nc.sync.dma_start(params[:, 0 : 3 * N], w_qkv.rearrange("(o r) n -> o (r n)", o=1))
        nc.scalar.dma_start(params[:, 3 * N : 6 * N], b_qkv.rearrange("(o r) n -> o (r n)", o=1))
        maps_q += load_maps(nc, held, xq, "xq", range(2, A))
        maps_k = load_maps(nc, held, xk, "xk", range(A))
        maps_v = load_maps(nc, held, xv, "xv", range(A))
        offsets = held.tile([PARTS, N // 16], U16, name="offsets")
        nc.sync.dma_start(offsets[:], offs)
        w_up_first = held.tile([PARTS, N], F32, name="w_up_first")
        nc.sync.dma_start(w_up_first[:], w_up[0:1, :].rearrange("o n -> (o n)").partition_broadcast(PARTS))
        w_up_cols = held.tile([PARTS, A * T], F32, name="w_up_cols")
        nc.scalar.dma_start(w_up_cols[:], w_up.rearrange("a (t p) -> p (a t)", p=PARTS))
        b_up_all = held.tile([PARTS, N], F32, name="b_up_all")
        nc.sync.dma_start(b_up_all[:], b_up.rearrange("o n -> (o n)").partition_broadcast(PARTS))
        base_blocks = base.rearrange("(a p h) s -> a h p s", a=A, h=H)
        out_blocks = out.rearrange("(a p h) s -> a h p s", a=A, h=H)
        windows = {}
        for h in range(H):
            for a in range(A):
                windows[a, h] = held.tile([PARTS, S], F32, name=f"window{a}{h}")
                nc.sync.dma_start(windows[a, h][:], base_blocks[a, h])

        spread = {}
        for r, label in enumerate(("q", "k")):
            spread[label] = banks.tile([PARTS, 2 * N], F32, name=f"spread_{label}", tag="bank")
            nc.tensor.matmul(spread[label][:, 0:N], ones[:], params[:, r * N : (r + 1) * N], start=True, stop=True)
            nc.tensor.matmul(
                spread[label][:, N : 2 * N], ones[:], params[:, (3 + r) * N : (4 + r) * N], start=True, stop=True
            )
        v_cols_psum = psum.tile([PARTS, 2 * T], F32, name="v_cols_psum")
        for t in range(T):
            gain_row = params[:, 2 * N + t * L : 2 * N + (t + 1) * L]
            bias_row = params[:, 5 * N + t * L : 5 * N + (t + 1) * L]
            nc.tensor.matmul(v_cols_psum[:, t : t + 1], gain_row, ones[:, 0:1], start=True, stop=True)
            nc.tensor.matmul(v_cols_psum[:, T + t : T + t + 1], bias_row, ones[:, 0:1], start=True, stop=True)
        v_cols = held.tile([PARTS, 2 * T], F32, name="v_cols")
        nc.scalar.copy(v_cols[:], v_cols_psum[:])

        q = gain_bias_rounded(nc, held, max_over_positions(nc, held, maps_q, "pooled_q"), spread["q"], "q")
        k = gain_bias_rounded(nc, held, max_over_positions(nc, held, maps_k, "pooled_k"), spread["k"], "k")

        attT = []
        for t in range(T):
            cluster = slice(t * L, (t + 1) * L)
            score = psum.tile([PARTS, L], F32, name=f"score{t}")
            for h in range(H):
                nc.tensor.matmul(score[:], q[:, h, cluster], k[:, h, cluster], start=(h == 0), stop=(h == H - 1))
            negmax = held.tile([PARTS, 1], F32, name=f"negmax{t}")
            nc.vector.tensor_reduce(negmax[:], score[:], AXIS.X, ALU.max, negate=True)
            e = held.tile([PARTS, L], F32, name=f"e{t}")
            esum = held.tile([PARTS, 1], F32, name=f"esum{t}")
            nc.scalar.activation(e[:], score[:], ACT.Exp, bias=negmax[:], scale=1.0, accum_out=esum[:])
            rsum = held.tile([PARTS, 1], F32, name=f"rsum{t}")
            nc.vector.reciprocal(rsum[:], esum[:])
            att = held.tile([PARTS, L], BF16, name=f"att{t}")
            nc.vector.tensor_scalar_mul(att[:], e[:], rsum[:])
            attT_psum = banks.tile([PARTS, L], BF16, name=f"attT_psum{t}", tag="bank")
            nc.tensor.transpose(attT_psum[:], att[:], ident_bf16[:])
            attT.append(held.tile([PARTS, L], BF16, name=f"attT{t}"))
            nc.vector.tensor_copy(attT[t][:], attT_psum[:])

        vT = []
        for h in range(H):
            pooled_v = held.tile([PARTS, N], F32, name=f"pooled_v{h}")
            nc.vector.tensor_max(pooled_v[:], maps_v[0][:, h, :], maps_v[1][:, h, :])
            for one in maps_v[2:]:
                nc.vector.tensor_max(pooled_v[:], pooled_v[:], one[:, h, :])
            vT_psum = psum.tile([PARTS, T, PARTS], F32, name=f"vT_psum{h}")
            vT.append(held.tile([PARTS, T, PARTS], BF16, name=f"vT{h}"))
            for t in range(T):
                nc.tensor.transpose(vT_psum[:, t, :], pooled_v[:, t * L : (t + 1) * L], ident_f32[:])
                nc.scalar.activation(
                    vT[h][:, t, :],
                    vT_psum[:, t, :],
                    ACT.Identity,
                    bias=v_cols[:, T + t : T + t + 1],
                    scale=v_cols[:, t : t + 1],
                )

        def place(a, h, product):
            nc.vector.tensor_tensor(windows[a, h][:].indirect(offsets[:]), product[:], b_up_all[:], ALU.add)
            nc.sync.dma_start(out_blocks[a, h], windows[a, h][:])

        product = ring.tile([PARTS, N], F32, name="product")
        for t in range(T):
            cluster = slice(t * L, (t + 1) * L)
            o = psum.tile([PARTS, L], F32, name=f"o{t}", tag=f"score{t}")
            nc.tensor.matmul(o[:], vT[0][:, t, :], attT[t][:], start=True, stop=True)
            nc.vector.tensor_tensor(product[:, cluster], o[:], w_up_first[:, cluster], ALU.mult)
        place(0, 0, product)

        for h in range(H):
            oT = psum.tile([PARTS, T, PARTS], F32, name=f"oT{h}", tag=f"vT_psum{h}")
            for t in range(T):
                nc.tensor.matmul(oT[:, t, :], attT[t][:], vT[h][:, t, :], start=True, stop=True)
            for a in range(A):
                if (a, h) == (0, 0):
                    continue
                product_psum = banks.tile([PARTS, N], F32, name="product_psum", tag="bank")
                for t in range(T):
                    scaledT = ring.tile([PARTS, PARTS], F32, name=f"scaledT{t}")
                    nc.scalar.mul(scaledT[:], oT[:, t, :], w_up_cols[:, a * T + t : a * T + t + 1])
                    nc.tensor.transpose(product_psum[:, t * L : (t + 1) * L], scaledT[:], ident_f32[:])
                product = ring.tile([PARTS, N], F32, name="product")
                nc.scalar.copy(product[:], product_psum[:])
                place(a, h, product)
